import numpy as np
import ml_dtypes


def mxq(x, axis, fmt="e4m3"):
    dtype, down = {"e4m3": (ml_dtypes.float8_e4m3fn, 7), "e5m2": (ml_dtypes.float8_e5m2, 14)}[fmt]
    v = np.moveaxis(np.asarray(x, np.float32).astype(ml_dtypes.bfloat16).astype(np.float64), axis, -1)
    blocks = v.reshape(v.shape[:-1] + (-1, 32))
    amax = np.abs(blocks).max(-1, keepdims=True)
    byte = np.maximum(np.where(amax > 0, np.frexp(amax)[1] - 1 + 127, 0) - down, 1)
    scale = np.exp2(byte - 127.0)
    codes = (blocks / scale).astype(np.float32).astype(dtype).astype(np.float64)
    return np.moveaxis((codes * scale).reshape(v.shape), -1, axis)


WIDE = False


def mx_kscale(k):
    if not WIDE:
        return np.ones(k)
    levels = np.array([10, -10, 5, -5, 0])
    a = np.random.permutation(np.resize(levels, k // 512 * 4)).reshape(k // 512, 4)
    idx = np.arange(k)
    return np.exp2(a[idx // 512, idx % 128 // 32])


BF16 = ml_dtypes.bfloat16


def bf(x):
    return np.asarray(x, np.float32).astype(BF16)


def f64(x):
    return np.asarray(x).astype(np.float64)


BATCH, ROWS, COLS, IN_DIM, OUT_DIM = 2, 32, 32, 512, 128
N = ROWS * COLS
EPS_BN = 1e-5
EPS_DEG = 1e-5


def _stencil9(x):
    R, C = x.shape[-3], x.shape[-2]
    pad = [(0, 0)] * (x.ndim - 3) + [(1, 1), (1, 1), (0, 0)]
    xp = np.pad(x, pad)
    out = np.zeros_like(x)
    for di in range(3):
        for dj in range(3):
            out = out + xp[..., di:di + R, dj:dj + C, :]
    return out


def _deg_inv_sqrt(rows, cols):
    D = _stencil9(np.ones((rows, cols, 1)))[..., 0]
    return (D + EPS_DEG) ** -0.5


def setup_inputs():
    s = mx_kscale(IN_DIM)
    mu = 0.5 * np.random.standard_normal(IN_DIM)
    bound = np.sqrt(6.0 / IN_DIM)
    return {"H": bf((np.random.standard_normal((BATCH, N, IN_DIM)) + mu) * s),
            "W": bf(np.random.uniform(-bound, bound, (IN_DIM, OUT_DIM)) / s[:, None]),
            "gamma": bf(1.0 + 0.1 * np.random.standard_normal(OUT_DIM)),
            "beta": bf(0.2 * np.random.standard_normal(OUT_DIM))}


def reference(H, W, gamma, beta):
    B, n_nodes, _ = H.shape
    Ht = mxq(f64(H), 2, "e4m3") @ mxq(f64(W), 0, "e4m3")
    mean = Ht.mean(axis=(0, 1))
    var = Ht.var(axis=(0, 1))
    Ht = (Ht - mean) * (1.0 / np.sqrt(var + EPS_BN)) * f64(gamma) + f64(beta)
    Ht = np.maximum(Ht, 0.0)
    d = _deg_inv_sqrt(ROWS, COLS)[None, :, :, None]
    Hg = Ht.reshape(B, ROWS, COLS, OUT_DIM)
    Hagg = d * _stencil9(Hg * d)
    return Hagg.reshape(B, n_nodes, OUT_DIM)

@@ -1,0 +1,225 @@
+import concourse.mybir as mybir
+from concourse.masks import make_identity
+
+F32 = mybir.dt.float32
+BF16 = mybir.dt.bfloat16
+U32 = mybir.dt.uint32
+U8 = mybir.dt.uint8
+FP8X4 = mybir.dt.float8_e4m3fn_x4
+ACT = mybir.ActivationFunctionType
+
+P = 128
+BATCH, ROWS, COLS, IN_DIM, OUT_DIM = 2, 32, 32, 512, 128
+NODES = BATCH * ROWS * COLS
+EPS_BN = 1e-5
+EPS_DEG = 1e-5
+
+FLOPS = 2 * NODES * IN_DIM * OUT_DIM
+
+CHUNK = 512
+CHUNKS = NODES // CHUNK
+CHUNK_ROWS = CHUNK // COLS
+PER_PART = CHUNK // P
+WORDS = IN_DIM // 2
+
+D_INSIDE = (9 + EPS_DEG) ** -0.5
+D_EDGE = (6 + EPS_DEG) ** -0.5
+D_CORNER = (4 + EPS_DEG) ** -0.5
+
+HALF_COLS = COLS // 2
+GROUP_ROWS = P // HALF_COLS
+GROUPS = NODES // (2 * P)
+GROUPS_PER_IMAGE = GROUPS // BATCH
+TOP, MIDDLE, BOTTOM = 0, 1, 2
+
+
+def group_kind(g):
+    if g % GROUPS_PER_IMAGE == 0:
+        return TOP
+    if g % GROUPS_PER_IMAGE == GROUPS_PER_IMAGE - 1:
+        return BOTTOM
+    return MIDDLE
+
+
+def tile_graphconvolutionbatch_s_kernel(tc, H, W, gamma, beta, out):
+    nc = tc.nc
+    h_rows = H.flatten_outer_dims()
+    out_groups = out.flatten_outer_dims().rearrange("(g p two) f -> p g (two f)", p=P, two=2)
+
+    with (
+        tc.tile_pool(name="keep", bufs=1) as keep,
+        tc.psum_pool(name="product", bufs=1) as product,
+        tc.psum_pool(name="turn", bufs=4) as turn,
+    ):
+        h_sb = keep.tile([P, CHUNKS * PER_PART * IN_DIM], BF16)
+        for j in range(CHUNKS):
+            nc.sync.dma_start(
+                out=h_sb[:, j * PER_PART * IN_DIM : (j + 1) * PER_PART * IN_DIM],
+                in_=h_rows[j * CHUNK : (j + 1) * CHUNK, :].rearrange("(p t) k -> p (t k)", t=PER_PART),
+            )
+        w_raw = keep.tile([P, 4, OUT_DIM], BF16)
+        nc.scalar.dma_start(
+            out=w_raw[:].rearrange("q (u e) c -> q u (e c)", u=2),
+            in_=W.rearrange("(u q e) c -> q u (e c)", u=2, e=2),
+        )
+        gamma_bf = keep.tile([P, 1], BF16)
+        beta_bf = keep.tile([P, 1], BF16)
+        nc.scalar.dma_start(out=gamma_bf[:], in_=gamma.rearrange("(p o) -> p o", o=1))
+        nc.scalar.dma_start(out=beta_bf[:], in_=beta.rearrange("(p o) -> p o", o=1))
+
+        ident = keep.tile([P, P], F32)
+        make_identity(nc, ident[:])
+        eps_bn = keep.tile([P, 1], F32)
+        eps_deg = keep.tile([P, 1], F32)
+        nc.vector.memset(eps_bn[:], EPS_BN)
+        nc.vector.memset(eps_deg[:], EPS_DEG)
+        table_warm = keep.tile([P, 1], F32)
+        nc.scalar.activation(out=table_warm[:], in_=eps_bn[:], func=ACT.Abs_reciprocal_sqrt)
+
+        relu_d = [keep.tile([P, ROWS, COLS + 2], F32, name="relu_d%d" % b) for b in range(BATCH)]
+        col_sums = [keep.tile([P, 2, ROWS + 2, HALF_COLS], F32, name="col_sums%d" % b) for b in range(BATCH)]
+        for b in range(BATCH):
+            nc.vector.memset(relu_d[b][:, :, 0 : COLS + 2 : COLS + 1], 0.0)
+            nc.vector.memset(col_sums[b][:, :, 0 : ROWS + 2 : ROWS + 1, :], 0.0)
+
+        degree = keep.tile([P, 3, 2, GROUP_ROWS, HALF_COLS], F32)
+        nc.vector.memset(degree[:], 9.0)
+        nc.vector.memset(degree[:, :, 0, :, 0], 6.0)
+        nc.vector.memset(degree[:, :, 1, :, HALF_COLS - 1], 6.0)
+        nc.vector.memset(degree[:, TOP, :, 0, :], 6.0)
+        nc.vector.memset(degree[:, BOTTOM, :, GROUP_ROWS - 1, :], 6.0)
+        for kind, row in ((TOP, 0), (BOTTOM, GROUP_ROWS - 1)):
+            nc.vector.memset(degree[:, kind, 0, row, 0:1], 4.0)
+            nc.vector.memset(degree[:, kind, 1, row, HALF_COLS - 1 : HALF_COLS], 4.0)
+        d_out = keep.tile([P, 3, 2], F32)
+        for kind in (TOP, MIDDLE, BOTTOM):
+            degree_t = turn.tile([P, 2, P], F32, tag="turn")
+            for par in range(2):
+                nc.tensor.transpose(
+                    degree_t[:, par, :], degree[:, kind, par, :, :].rearrange("f r m -> f (r m)"), ident[:]
+                )
+            nc.scalar.activation(
+                out=d_out[:, kind, :], in_=degree_t[:, :, 0], func=ACT.Abs_reciprocal_sqrt, bias=eps_deg[:]
+            )
+
+        w_grouped = keep.tile([P, OUT_DIM, 4], BF16, align_bytes=64)
+        w_codes = keep.tile([P, OUT_DIM], U32, align_bytes=64)
+        w_scales = keep.tile([P, OUT_DIM], U8, align_bytes=64)
+        nc.vector.tensor_copy(out=w_grouped[:], in_=w_raw[:].rearrange("q t c -> q c t"))
+        nc.vector.quantize_mx(
+            out=w_codes[:].bitcast(FP8X4), scales=w_scales[:], in_=w_grouped[:].rearrange("q c t -> q (c t)")
+        )
+
+        gamma_d = keep.tile([P, 2], F32)
+        beta_d = keep.tile([P, 1], F32)
+        nc.vector.tensor_scalar_mul(out=gamma_d[:, 0:1], in0=gamma_bf[:], scalar1=D_INSIDE)
+        nc.vector.tensor_scalar_mul(out=gamma_d[:, 1:2], in0=gamma_bf[:], scalar1=-D_INSIDE)
+        nc.vector.tensor_scalar_mul(out=beta_d[:], in0=beta_bf[:], scalar1=D_INSIDE)
+
+        h_words = h_sb[:].bitcast(F32).rearrange("p (j t u w) -> p j t u w", j=CHUNKS, t=PER_PART, u=2)
+        h_grouped = keep.tile([P, NODES * 4], BF16, align_bytes=64)
+        h_grouped_words = h_grouped[:].bitcast(F32).rearrange(
+            "q (j t p u) -> q j t p u", j=CHUNKS, t=PER_PART, u=2
+        )
+        h_codes = keep.tile([P, NODES], U32, align_bytes=64)
+        h_scales = keep.tile([P, NODES], U8, align_bytes=64)
+        stats = keep.tile([P, CHUNKS, 6], F32)
+        y = [product.tile([P, CHUNK], F32, name="y%d" % j) for j in range(CHUNKS)]
+        half = CHUNK // 2
+        for j in range(CHUNKS):
+            for h in range(2):
+                h_t = turn.tile([P, 2, 2, P], F32, tag="turn")
+                for t in range(2):
+                    for u in range(2):
+                        nc.tensor.transpose(h_t[:, t, u, :], h_words[:, j, 2 * h + t, u, :], ident[:])
+                nc.scalar.copy(
+                    out=h_grouped_words[:, j, 2 * h : 2 * h + 2, :, :],
+                    in_=h_t[:].rearrange("q t u p -> q t p u"),
+                )
+                first = j * CHUNK + h * half
+                nc.vector.quantize_mx(
+                    out=h_codes[:, first : first + half].bitcast(FP8X4),
+                    scales=h_scales[:, first : first + half],
+                    in_=h_grouped[:, 4 * first : 4 * (first + half)],
+                )
+            nc.tensor.matmul_mx(
+                out=y[j][:],
+                lhsT=w_codes[:].bitcast(FP8X4),
+                lhsT_scale=w_scales[:],
+                rhs=h_codes[:, j * CHUNK : (j + 1) * CHUNK].bitcast(FP8X4),
+                rhs_scale=h_scales[:, j * CHUNK : (j + 1) * CHUNK],
+                start=True,
+                stop=True,
+            )
+            nc.vector.bn_stats(out=stats[:, j, :], in_=y[j][:])
+
+        mean_var = keep.tile([P, 2], F32)
+        nc.vector.bn_aggr(out=mean_var[:], in_=stats[:].rearrange("f j s -> f (j s)"))
+        rstd = keep.tile([P, 1], F32)
+        scale = keep.tile([P, 2], F32)
+        bias = keep.tile([P, 1], F32)
+        nc.scalar.activation(out=rstd[:], in_=mean_var[:, 1:2], func=ACT.Abs_reciprocal_sqrt, bias=eps_bn[:])
+        nc.scalar.activation(out=scale[:], in_=gamma_d[:], func=ACT.Copy, scale=rstd[:])
+        nc.scalar.activation(
+            out=bias[:], in_=mean_var[:, 0:1], func=ACT.Identity, scale=scale[:, 1:2], bias=beta_d[:]
+        )
+
+        pair = keep.tile([P, BATCH, ROWS, HALF_COLS], F32)
+        out_sb = keep.tile([P, GROUPS, 2, OUT_DIM], F32)
+        last = COLS + 1
+        for b in range(BATCH):
+            x = relu_d[b]
+            for hh in range(2):
+                rows = slice(hh * CHUNK_ROWS, (hh + 1) * CHUNK_ROWS)
+                nc.scalar.activation(
+                    out=x[:, rows, 1:last].rearrange("f r (q t) -> f r q t", t=PER_PART),
+                    in_=y[2 * b + hh][:].rearrange("f (t r q) -> f r q t", t=PER_PART, r=CHUNK_ROWS),
+                    func=ACT.Relu,
+                    scale=scale[:, 0:1],
+                    bias=bias[:],
+                )
+            nc.scalar.mul(
+                out=x[:, 0 : ROWS : ROWS - 1, 2 : last - 1],
+                in_=x[:, 0 : ROWS : ROWS - 1, 2 : last - 1],
+                mul=D_EDGE / D_INSIDE,
+            )
+            nc.scalar.mul(
+                out=x[:, 1 : ROWS - 1, 1 : last : COLS - 1],
+                in_=x[:, 1 : ROWS - 1, 1 : last : COLS - 1],
+                mul=D_EDGE / D_INSIDE,
+            )
+            nc.scalar.mul(
+                out=x[:, 0 : ROWS : ROWS - 1, 1 : last : COLS - 1],
+                in_=x[:, 0 : ROWS : ROWS - 1, 1 : last : COLS - 1],
+                mul=D_CORNER / D_INSIDE,
+            )
+            for hh in range(2):
+                rows = slice(hh * CHUNK_ROWS, (hh + 1) * CHUNK_ROWS)
+                padded_rows = slice(1 + hh * CHUNK_ROWS, 1 + (hh + 1) * CHUNK_ROWS)
+                nc.vector.tensor_add(out=pair[:, b, rows, :], in0=x[:, rows, 1:last:2], in1=x[:, rows, 2 : last + 1 : 2])
+                nc.vector.tensor_add(
+                    out=col_sums[b][:, 0, padded_rows, :], in0=pair[:, b, rows, :], in1=x[:, rows, 0 : last - 1 : 2]
+                )
+                nc.vector.tensor_add(
+                    out=col_sums[b][:, 1, padded_rows, :], in0=pair[:, b, rows, :], in1=x[:, rows, 3 : last + 1 : 2]
+                )
+            for g in range(b * GROUPS_PER_IMAGE, (b + 1) * GROUPS_PER_IMAGE):
+                top = (g % GROUPS_PER_IMAGE) * GROUP_ROWS
+                box_t = turn.tile([P, 2, OUT_DIM], F32, tag="turn")
+                for par in range(2):
+                    for dr in range(3):
+                        nc.tensor.matmul(
+                            out=box_t[:, par, :],
+                            lhsT=col_sums[b][:, par, top + dr : top + dr + GROUP_ROWS, :].rearrange("f r m -> f (r m)"),
+                            rhs=ident[:],
+                            is_transpose=True,
+                            start=(dr == 0),
+                            stop=(dr == 2),
+                        )
+                for par in range(2):
+                    d_col = d_out[:, group_kind(g), par : par + 1]
+                    if g % 2 == 0:
+                        nc.scalar.activation(out=out_sb[:, g, par, :], in_=box_t[:, par, :], func=ACT.Copy, scale=d_col)
+                    else:
+                        nc.vector.tensor_scalar_mul(out=out_sb[:, g, par, :], in0=box_t[:, par, :], scalar1=d_col)
+                nc.sync.dma_start(out=out_groups[:, g, :], in_=out_sb[:, g, :, :].rearrange("p two f -> p (two f)"))

@@ -48,24 +48,27 @@ def tile_graphconvolutionbatch_s_kernel(tc, H, W, gamma, beta, out):
 
     with (
         tc.tile_pool(name="keep", bufs=1) as keep,
-        tc.psum_pool(name="product", bufs=1) as product,
-        tc.psum_pool(name="turn", bufs=4) as turn,
+        tc.psum_pool(name="psum", bufs=8) as psum,
+        tc.manual_schedule(),
     ):
-        h_sb = keep.tile([P, CHUNKS * PER_PART * IN_DIM], BF16)
-        for j in range(CHUNKS):
-            nc.sync.dma_start(
-                out=h_sb[:, j * PER_PART * IN_DIM : (j + 1) * PER_PART * IN_DIM],
-                in_=h_rows[j * CHUNK : (j + 1) * CHUNK, :].rearrange("(p t) k -> p (t k)", t=PER_PART),
-            )
         w_raw = keep.tile([P, 4, OUT_DIM], BF16)
         nc.scalar.dma_start(
             out=w_raw[:].rearrange("q (u e) c -> q u (e c)", u=2),
             in_=W.rearrange("(u q e) c -> q u (e c)", u=2, e=2),
         )
+        h_sb = keep.tile([P, CHUNKS * PER_PART * IN_DIM], BF16)
+        for j in range(CHUNKS):
+            chunk_rows = h_rows[j * CHUNK : (j + 1) * CHUNK, :].rearrange("(p t) k -> p t k", t=PER_PART)
+            for h in range(2):
+                first_col = (j * PER_PART + 2 * h) * IN_DIM
+                nc.sync.dma_start(
+                    out=h_sb[:, first_col : first_col + 2 * IN_DIM],
+                    in_=chunk_rows[:, 2 * h : 2 * h + 2, :].rearrange("p t k -> p (t k)"),
+                )
         gamma_bf = keep.tile([P, 1], BF16)
         beta_bf = keep.tile([P, 1], BF16)
-        nc.scalar.dma_start(out=gamma_bf[:], in_=gamma.rearrange("(p o) -> p o", o=1))
-        nc.scalar.dma_start(out=beta_bf[:], in_=beta.rearrange("(p o) -> p o", o=1))
+        nc.sync.dma_start(out=gamma_bf[:], in_=gamma.rearrange("(p o) -> p o", o=1))
+        nc.sync.dma_start(out=beta_bf[:], in_=beta.rearrange("(p o) -> p o", o=1))
 
         ident = keep.tile([P, P], F32)
         make_identity(nc, ident[:])
@@ -82,25 +85,15 @@ def tile_graphconvolutionbatch_s_kernel(tc, H, W, gamma, beta, out):
             nc.vector.memset(relu_d[b][:, :, 0 : COLS + 2 : COLS + 1], 0.0)
             nc.vector.memset(col_sums[b][:, :, 0 : ROWS + 2 : ROWS + 1, :], 0.0)
 
-        degree = keep.tile([P, 3, 2, GROUP_ROWS, HALF_COLS], F32)
+        degree = keep.tile([P, 2, 3, GROUP_ROWS, HALF_COLS], F32)
         nc.vector.memset(degree[:], 9.0)
-        nc.vector.memset(degree[:, :, 0, :, 0], 6.0)
-        nc.vector.memset(degree[:, :, 1, :, HALF_COLS - 1], 6.0)
-        nc.vector.memset(degree[:, TOP, :, 0, :], 6.0)
-        nc.vector.memset(degree[:, BOTTOM, :, GROUP_ROWS - 1, :], 6.0)
+        nc.vector.memset(degree[:, 0, :, :, 0], 6.0)
+        nc.vector.memset(degree[:, 1, :, :, HALF_COLS - 1], 6.0)
+        nc.vector.memset(degree[:, :, TOP, 0, :], 6.0)
+        nc.vector.memset(degree[:, :, BOTTOM, GROUP_ROWS - 1, :], 6.0)
         for kind, row in ((TOP, 0), (BOTTOM, GROUP_ROWS - 1)):
-            nc.vector.memset(degree[:, kind, 0, row, 0:1], 4.0)
-            nc.vector.memset(degree[:, kind, 1, row, HALF_COLS - 1 : HALF_COLS], 4.0)
-        d_out = keep.tile([P, 3, 2], F32)
-        for kind in (TOP, MIDDLE, BOTTOM):
-            degree_t = turn.tile([P, 2, P], F32, tag="turn")
-            for par in range(2):
-                nc.tensor.transpose(
-                    degree_t[:, par, :], degree[:, kind, par, :, :].rearrange("f r m -> f (r m)"), ident[:]
-                )
-            nc.scalar.activation(
-                out=d_out[:, kind, :], in_=degree_t[:, :, 0], func=ACT.Abs_reciprocal_sqrt, bias=eps_deg[:]
-            )
+            nc.vector.memset(degree[:, 0, kind, row, 0:1], 4.0)
+            nc.vector.memset(degree[:, 1, kind, row, HALF_COLS - 1 : HALF_COLS], 4.0)
 
         w_grouped = keep.tile([P, OUT_DIM, 4], BF16, align_bytes=64)
         w_codes = keep.tile([P, OUT_DIM], U32, align_bytes=64)
@@ -110,12 +103,6 @@ def tile_graphconvolutionbatch_s_kernel(tc, H, W, gamma, beta, out):
             out=w_codes[:].bitcast(FP8X4), scales=w_scales[:], in_=w_grouped[:].rearrange("q c t -> q (c t)")
         )
 
-        gamma_d = keep.tile([P, 2], F32)
-        beta_d = keep.tile([P, 1], F32)
-        nc.vector.tensor_scalar_mul(out=gamma_d[:, 0:1], in0=gamma_bf[:], scalar1=D_INSIDE)
-        nc.vector.tensor_scalar_mul(out=gamma_d[:, 1:2], in0=gamma_bf[:], scalar1=-D_INSIDE)
-        nc.vector.tensor_scalar_mul(out=beta_d[:], in0=beta_bf[:], scalar1=D_INSIDE)
-
         h_words = h_sb[:].bitcast(F32).rearrange("p (j t u w) -> p j t u w", j=CHUNKS, t=PER_PART, u=2)
         h_grouped = keep.tile([P, NODES * 4], BF16, align_bytes=64)
         h_grouped_words = h_grouped[:].bitcast(F32).rearrange(
@@ -124,11 +111,12 @@ def tile_graphconvolutionbatch_s_kernel(tc, H, W, gamma, beta, out):
         h_codes = keep.tile([P, NODES], U32, align_bytes=64)
         h_scales = keep.tile([P, NODES], U8, align_bytes=64)
         stats = keep.tile([P, CHUNKS, 6], F32)
-        y = [product.tile([P, CHUNK], F32, name="y%d" % j) for j in range(CHUNKS)]
+        y = []
         half = CHUNK // 2
-        for j in range(CHUNKS):
+
+        def turn_and_quantise(j):
             for h in range(2):
-                h_t = turn.tile([P, 2, 2, P], F32, tag="turn")
+                h_t = psum.tile([P, 2, 2, P], F32, tag="bank")
                 for t in range(2):
                     for u in range(2):
                         nc.tensor.transpose(h_t[:, t, u, :], h_words[:, j, 2 * h + t, u, :], ident[:])
@@ -142,6 +130,9 @@ def tile_graphconvolutionbatch_s_kernel(tc, H, W, gamma, beta, out):
                     scales=h_scales[:, first : first + half],
                     in_=h_grouped[:, 4 * first : 4 * (first + half)],
                 )
+
+        def multiply(j):
+            y.append(psum.tile([P, CHUNK], F32, tag="bank", name="y%d" % j))
             nc.tensor.matmul_mx(
                 out=y[j][:],
                 lhsT=w_codes[:].bitcast(FP8X4),
@@ -152,6 +143,24 @@ def tile_graphconvolutionbatch_s_kernel(tc, H, W, gamma, beta, out):
                 stop=True,
             )
             nc.vector.bn_stats(out=stats[:, j, :], in_=y[j][:])
+
+        for j in range(CHUNKS):
+            turn_and_quantise(j)
+            if j > 0:
+                multiply(j - 1)
+        gamma_d = keep.tile([P, 2], F32)
+        beta_d = keep.tile([P, 1], F32)
+        nc.vector.tensor_scalar_mul(out=gamma_d[:, 0:1], in0=gamma_bf[:], scalar1=D_INSIDE)
+        nc.vector.tensor_scalar_mul(out=gamma_d[:, 1:2], in0=gamma_bf[:], scalar1=-D_INSIDE)
+        nc.vector.tensor_scalar_mul(out=beta_d[:], in0=beta_bf[:], scalar1=D_INSIDE)
+        multiply(CHUNKS - 1)
+
+        degree_t = [psum.tile([P, 3, P], F32, tag="bank", name="degree_t%d" % par) for par in range(2)]
+        for par in range(2):
+            for kind in (TOP, MIDDLE, BOTTOM):
+                nc.tensor.transpose(
+                    degree_t[par][:, kind, :], degree[:, par, kind, :, :].rearrange("f r m -> f (r m)"), ident[:]
+                )
 
         mean_var = keep.tile([P, 2], F32)
         nc.vector.bn_aggr(out=mean_var[:], in_=stats[:].rearrange("f j s -> f (j s)"))
@@ -164,62 +173,69 @@ def tile_graphconvolutionbatch_s_kernel(tc, H, W, gamma, beta, out):
             out=bias[:], in_=mean_var[:, 0:1], func=ACT.Identity, scale=scale[:, 1:2], bias=beta_d[:]
         )
 
-        pair = keep.tile([P, BATCH, ROWS, HALF_COLS], F32)
-        out_sb = keep.tile([P, GROUPS, 2, OUT_DIM], F32)
         last = COLS + 1
-        for b in range(BATCH):
-            x = relu_d[b]
-            for hh in range(2):
-                rows = slice(hh * CHUNK_ROWS, (hh + 1) * CHUNK_ROWS)
-                nc.scalar.activation(
-                    out=x[:, rows, 1:last].rearrange("f r (q t) -> f r q t", t=PER_PART),
-                    in_=y[2 * b + hh][:].rearrange("f (t r q) -> f r q t", t=PER_PART, r=CHUNK_ROWS),
-                    func=ACT.Relu,
-                    scale=scale[:, 0:1],
-                    bias=bias[:],
-                )
-            nc.scalar.mul(
-                out=x[:, 0 : ROWS : ROWS - 1, 2 : last - 1],
-                in_=x[:, 0 : ROWS : ROWS - 1, 2 : last - 1],
-                mul=D_EDGE / D_INSIDE,
+        for j in range(CHUNKS):
+            rows = slice((j % 2) * CHUNK_ROWS, (j % 2 + 1) * CHUNK_ROWS)
+            nc.scalar.activation(
+                out=relu_d[j // 2][:, rows, 1:last].rearrange("f r (q t) -> f r q t", t=PER_PART),
+                in_=y[j][:].rearrange("f (t r q) -> f r q t", t=PER_PART, r=CHUNK_ROWS),
+                func=ACT.Relu,
+                scale=scale[:, 0:1],
+                bias=bias[:],
             )
-            nc.scalar.mul(
-                out=x[:, 1 : ROWS - 1, 1 : last : COLS - 1],
-                in_=x[:, 1 : ROWS - 1, 1 : last : COLS - 1],
-                mul=D_EDGE / D_INSIDE,
+        d_out = keep.tile([P, 3, 2], F32)
+        for par in range(2):
+            nc.scalar.activation(
+                out=d_out[:, :, par], in_=degree_t[par][:, :, 0], func=ACT.Abs_reciprocal_sqrt, bias=eps_deg[:]
             )
-            nc.scalar.mul(
-                out=x[:, 0 : ROWS : ROWS - 1, 1 : last : COLS - 1],
-                in_=x[:, 0 : ROWS : ROWS - 1, 1 : last : COLS - 1],
-                mul=D_CORNER / D_INSIDE,
+
+        pair = keep.tile([P, CHUNKS, CHUNK_ROWS, HALF_COLS], F32)
+
+        def border(j):
+            x = relu_d[j // 2]
+            edge_row = 0 if j % 2 == 0 else ROWS - 1
+            other_rows = slice(1, CHUNK_ROWS) if j % 2 == 0 else slice(CHUNK_ROWS, ROWS - 1)
+            for region, factor in (
+                (x[:, edge_row, 2 : last - 1], D_EDGE / D_INSIDE),
+                (x[:, other_rows, 1 : last : COLS - 1], D_EDGE / D_INSIDE),
+                (x[:, edge_row, 1 : last : COLS - 1], D_CORNER / D_INSIDE),
+            ):
+                nc.vector.tensor_scalar_mul(out=region, in0=region, scalar1=factor)
+
+        border(0)
+        for j in range(CHUNKS):
+            x = relu_d[j // 2]
+            rows = slice((j % 2) * CHUNK_ROWS, (j % 2 + 1) * CHUNK_ROWS)
+            padded_rows = slice(1 + (j % 2) * CHUNK_ROWS, 1 + (j % 2 + 1) * CHUNK_ROWS)
+            nc.vector.tensor_add(out=pair[:, j, :, :], in0=x[:, rows, 1:last:2], in1=x[:, rows, 2 : last + 1 : 2])
+            if j + 1 < CHUNKS:
+                border(j + 1)
+            nc.vector.tensor_add(
+                out=col_sums[j // 2][:, 0, padded_rows, :], in0=pair[:, j, :, :], in1=x[:, rows, 0 : last - 1 : 2]
             )
-            for hh in range(2):
-                rows = slice(hh * CHUNK_ROWS, (hh + 1) * CHUNK_ROWS)
-                padded_rows = slice(1 + hh * CHUNK_ROWS, 1 + (hh + 1) * CHUNK_ROWS)
-                nc.vector.tensor_add(out=pair[:, b, rows, :], in0=x[:, rows, 1:last:2], in1=x[:, rows, 2 : last + 1 : 2])
-                nc.vector.tensor_add(
-                    out=col_sums[b][:, 0, padded_rows, :], in0=pair[:, b, rows, :], in1=x[:, rows, 0 : last - 1 : 2]
-                )
-                nc.vector.tensor_add(
-                    out=col_sums[b][:, 1, padded_rows, :], in0=pair[:, b, rows, :], in1=x[:, rows, 3 : last + 1 : 2]
-                )
-            for g in range(b * GROUPS_PER_IMAGE, (b + 1) * GROUPS_PER_IMAGE):
-                top = (g % GROUPS_PER_IMAGE) * GROUP_ROWS
-                box_t = turn.tile([P, 2, OUT_DIM], F32, tag="turn")
-                for par in range(2):
-                    for dr in range(3):
-                        nc.tensor.matmul(
-                            out=box_t[:, par, :],
-                            lhsT=col_sums[b][:, par, top + dr : top + dr + GROUP_ROWS, :].rearrange("f r m -> f (r m)"),
-                            rhs=ident[:],
-                            is_transpose=True,
-                            start=(dr == 0),
-                            stop=(dr == 2),
-                        )
-                for par in range(2):
-                    d_col = d_out[:, group_kind(g), par : par + 1]
-                    if g % 2 == 0:
-                        nc.scalar.activation(out=out_sb[:, g, par, :], in_=box_t[:, par, :], func=ACT.Copy, scale=d_col)
-                    else:
-                        nc.vector.tensor_scalar_mul(out=out_sb[:, g, par, :], in0=box_t[:, par, :], scalar1=d_col)
-                nc.sync.dma_start(out=out_groups[:, g, :], in_=out_sb[:, g, :, :].rearrange("p two f -> p (two f)"))
+            nc.vector.tensor_add(
+                out=col_sums[j // 2][:, 1, padded_rows, :], in0=pair[:, j, :, :], in1=x[:, rows, 3 : last + 1 : 2]
+            )
+
+        out_sb = keep.tile([P, GROUPS, 2, OUT_DIM], F32)
+        for g in range(GROUPS):
+            top = (g % GROUPS_PER_IMAGE) * GROUP_ROWS
+            for par in range(2):
+                box_t = psum.tile([P, OUT_DIM], F32, tag="bank")
+                for dr in range(3):
+                    nc.tensor.matmul(
+                        out=box_t[:],
+                        lhsT=col_sums[g // GROUPS_PER_IMAGE][:, par, top + dr : top + dr + GROUP_ROWS, :].rearrange(
+                            "f r m -> f (r m)"
+                        ),
+                        rhs=ident[:],
+                        is_transpose=True,
+                        start=(dr == 0),
+                        stop=(dr == 2),
+                    )
+                d_col = d_out[:, group_kind(g), par : par + 1]
+                if par == 0:
+                    nc.scalar.activation(out=out_sb[:, g, par, :], in_=box_t[:], func=ACT.Copy, scale=d_col)
+                else:
+                    nc.vector.tensor_scalar_mul(out=out_sb[:, g, par, :], in0=box_t[:], scalar1=d_col)
+            nc.sync.dma_start(out=out_groups[:, g, :], in_=out_sb[:, g, :, :].rearrange("p two f -> p (two f)"))

@@ -146,14 +146,14 @@ def tile_graphconvolutionbatch_s_kernel(tc, H, W, gamma, beta, out):
 
         for j in range(CHUNKS):
             turn_and_quantise(j)
-            if j > 0:
-                multiply(j - 1)
+        for j in range(CHUNKS):
+            multiply(j)
+
         gamma_d = keep.tile([P, 2], F32)
         beta_d = keep.tile([P, 1], F32)
-        nc.vector.tensor_scalar_mul(out=gamma_d[:, 0:1], in0=gamma_bf[:], scalar1=D_INSIDE)
-        nc.vector.tensor_scalar_mul(out=gamma_d[:, 1:2], in0=gamma_bf[:], scalar1=-D_INSIDE)
-        nc.vector.tensor_scalar_mul(out=beta_d[:], in0=beta_bf[:], scalar1=D_INSIDE)
-        multiply(CHUNKS - 1)
+        nc.gpsimd.tensor_scalar_mul(out=gamma_d[:, 0:1], in0=gamma_bf[:], scalar1=D_INSIDE)
+        nc.gpsimd.tensor_scalar_mul(out=gamma_d[:, 1:2], in0=gamma_bf[:], scalar1=-D_INSIDE)
+        nc.gpsimd.tensor_scalar_mul(out=beta_d[:], in0=beta_bf[:], scalar1=D_INSIDE)
 
         degree_t = [psum.tile([P, 3, P], F32, tag="bank", name="degree_t%d" % par) for par in range(2)]
         for par in range(2):
@@ -208,11 +208,11 @@ def tile_graphconvolutionbatch_s_kernel(tc, H, W, gamma, beta, out):
             rows = slice((j % 2) * CHUNK_ROWS, (j % 2 + 1) * CHUNK_ROWS)
             padded_rows = slice(1 + (j % 2) * CHUNK_ROWS, 1 + (j % 2 + 1) * CHUNK_ROWS)
             nc.vector.tensor_add(out=pair[:, j, :, :], in0=x[:, rows, 1:last:2], in1=x[:, rows, 2 : last + 1 : 2])
-            if j + 1 < CHUNKS:
-                border(j + 1)
             nc.vector.tensor_add(
                 out=col_sums[j // 2][:, 0, padded_rows, :], in0=pair[:, j, :, :], in1=x[:, rows, 0 : last - 1 : 2]
             )
+            if j + 1 < CHUNKS:
+                border(j + 1)
             nc.vector.tensor_add(
                 out=col_sums[j // 2][:, 1, padded_rows, :], in0=pair[:, j, :, :], in1=x[:, rows, 3 : last + 1 : 2]
             )

@@ -7,6 +7,7 @@ U32 = mybir.dt.uint32
 U8 = mybir.dt.uint8
 FP8X4 = mybir.dt.float8_e4m3fn_x4
 ACT = mybir.ActivationFunctionType
+ALU = mybir.AluOpType
 
 P = 128
 BATCH, ROWS, COLS, IN_DIM, OUT_DIM = 2, 32, 32, 512, 128
@@ -149,10 +150,11 @@ def tile_graphconvolutionbatch_s_kernel(tc, H, W, gamma, beta, out):
         for j in range(CHUNKS):
             multiply(j)
 
-        gamma_d = keep.tile([P, 2], F32)
+        gamma_d = keep.tile([P, 1], F32)
+        minus_gamma_d = keep.tile([P, 1], F32)
         beta_d = keep.tile([P, 1], F32)
-        nc.gpsimd.tensor_scalar_mul(out=gamma_d[:, 0:1], in0=gamma_bf[:], scalar1=D_INSIDE)
-        nc.gpsimd.tensor_scalar_mul(out=gamma_d[:, 1:2], in0=gamma_bf[:], scalar1=-D_INSIDE)
+        nc.gpsimd.tensor_scalar_mul(out=gamma_d[:], in0=gamma_bf[:], scalar1=D_INSIDE)
+        nc.gpsimd.tensor_scalar_mul(out=minus_gamma_d[:], in0=gamma_bf[:], scalar1=-D_INSIDE)
         nc.gpsimd.tensor_scalar_mul(out=beta_d[:], in0=beta_bf[:], scalar1=D_INSIDE)
 
         degree_t = [psum.tile([P, 3, P], F32, tag="bank", name="degree_t%d" % par) for par in range(2)]
@@ -165,12 +167,14 @@ def tile_graphconvolutionbatch_s_kernel(tc, H, W, gamma, beta, out):
         mean_var = keep.tile([P, 2], F32)
         nc.vector.bn_aggr(out=mean_var[:], in_=stats[:].rearrange("f j s -> f (j s)"))
         rstd = keep.tile([P, 1], F32)
-        scale = keep.tile([P, 2], F32)
+        minus_mean_gamma_d = keep.tile([P, 1], F32)
+        scale = keep.tile([P, 1], F32)
         bias = keep.tile([P, 1], F32)
         nc.scalar.activation(out=rstd[:], in_=mean_var[:, 1:2], func=ACT.Abs_reciprocal_sqrt, bias=eps_bn[:])
-        nc.scalar.activation(out=scale[:], in_=gamma_d[:], func=ACT.Copy, scale=rstd[:])
-        nc.scalar.activation(
-            out=bias[:], in_=mean_var[:, 0:1], func=ACT.Identity, scale=scale[:, 1:2], bias=beta_d[:]
+        nc.vector.tensor_mul(out=minus_mean_gamma_d[:], in0=mean_var[:, 0:1], in1=minus_gamma_d[:])
+        nc.vector.tensor_mul(out=scale[:], in0=gamma_d[:], in1=rstd[:])
+        nc.vector.scalar_tensor_tensor(
+            out=bias[:], in0=minus_mean_gamma_d[:], scalar=rstd[:], in1=beta_d[:], op0=ALU.mult, op1=ALU.add
         )
 
         last = COLS + 1
@@ -180,7 +184,7 @@ def tile_graphconvolutionbatch_s_kernel(tc, H, W, gamma, beta, out):
                 out=relu_d[j // 2][:, rows, 1:last].rearrange("f r (q t) -> f r q t", t=PER_PART),
                 in_=y[j][:].rearrange("f (t r q) -> f r q t", t=PER_PART, r=CHUNK_ROWS),
                 func=ACT.Relu,
-                scale=scale[:, 0:1],
+                scale=scale[:],
                 bias=bias[:],
             )
         d_out = keep.tile([P, 3, 2], F32)

import concourse.mybir as mybir
from concourse.masks import make_identity

F32 = mybir.dt.float32
BF16 = mybir.dt.bfloat16
U32 = mybir.dt.uint32
U8 = mybir.dt.uint8
FP8X4 = mybir.dt.float8_e4m3fn_x4
ACT = mybir.ActivationFunctionType
ALU = mybir.AluOpType

P = 128
BATCH, ROWS, COLS, IN_DIM, OUT_DIM = 2, 32, 32, 512, 128
NODES = BATCH * ROWS * COLS
EPS_BN = 1e-5
EPS_DEG = 1e-5

FLOPS = 2 * NODES * IN_DIM * OUT_DIM

CHUNK = 512
CHUNKS = NODES // CHUNK
CHUNK_ROWS = CHUNK // COLS
PER_PART = CHUNK // P
WORDS = IN_DIM // 2

D_INSIDE = (9 + EPS_DEG) ** -0.5
D_EDGE = (6 + EPS_DEG) ** -0.5
D_CORNER = (4 + EPS_DEG) ** -0.5

HALF_COLS = COLS // 2
GROUP_ROWS = P // HALF_COLS
GROUPS = NODES // (2 * P)
GROUPS_PER_IMAGE = GROUPS // BATCH
TOP, MIDDLE, BOTTOM = 0, 1, 2


def group_kind(g):
    if g % GROUPS_PER_IMAGE == 0:
        return TOP
    if g % GROUPS_PER_IMAGE == GROUPS_PER_IMAGE - 1:
        return BOTTOM
    return MIDDLE


def tile_graphconvolutionbatch_s_kernel(tc, H, W, gamma, beta, out):
    nc = tc.nc
    h_rows = H.flatten_outer_dims()
    out_groups = out.flatten_outer_dims().rearrange("(g p two) f -> p g (two f)", p=P, two=2)

    with (
        tc.tile_pool(name="keep", bufs=1) as keep,
        tc.psum_pool(name="psum", bufs=8) as psum,
        tc.manual_schedule(),
    ):
        w_raw = keep.tile([P, 4, OUT_DIM], BF16)
        nc.scalar.dma_start(
            out=w_raw[:].rearrange("q (u e) c -> q u (e c)", u=2),
            in_=W.rearrange("(u q e) c -> q u (e c)", u=2, e=2),
        )
        h_sb = keep.tile([P, CHUNKS * PER_PART * IN_DIM], BF16)
        for j in range(CHUNKS):
            chunk_rows = h_rows[j * CHUNK : (j + 1) * CHUNK, :].rearrange("(p t) k -> p t k", t=PER_PART)
            for h in range(2):
                first_col = (j * PER_PART + 2 * h) * IN_DIM
                nc.sync.dma_start(
                    out=h_sb[:, first_col : first_col + 2 * IN_DIM],
                    in_=chunk_rows[:, 2 * h : 2 * h + 2, :].rearrange("p t k -> p (t k)"),
                )
        gamma_bf = keep.tile([P, 1], BF16)
        beta_bf = keep.tile([P, 1], BF16)
        nc.sync.dma_start(out=gamma_bf[:], in_=gamma.rearrange("(p o) -> p o", o=1))
        nc.sync.dma_start(out=beta_bf[:], in_=beta.rearrange("(p o) -> p o", o=1))

        ident = keep.tile([P, P], F32)
        make_identity(nc, ident[:])
        eps_bn = keep.tile([P, 1], F32)
        eps_deg = keep.tile([P, 1], F32)
        nc.vector.memset(eps_bn[:], EPS_BN)
        nc.vector.memset(eps_deg[:], EPS_DEG)
        table_warm = keep.tile([P, 1], F32)
        nc.scalar.activation(out=table_warm[:], in_=eps_bn[:], func=ACT.Abs_reciprocal_sqrt)

        relu_d = [keep.tile([P, ROWS, COLS + 2], F32, name="relu_d%d" % b) for b in range(BATCH)]
        col_sums = [keep.tile([P, 2, ROWS + 2, HALF_COLS], F32, name="col_sums%d" % b) for b in range(BATCH)]
        for b in range(BATCH):
            nc.vector.memset(relu_d[b][:, :, 0 : COLS + 2 : COLS + 1], 0.0)
            nc.vector.memset(col_sums[b][:, :, 0 : ROWS + 2 : ROWS + 1, :], 0.0)

        degree = keep.tile([P, 2, 3, GROUP_ROWS, HALF_COLS], F32)
        nc.vector.memset(degree[:], 9.0)
        nc.vector.memset(degree[:, 0, :, :, 0], 6.0)
        nc.vector.memset(degree[:, 1, :, :, HALF_COLS - 1], 6.0)
        nc.vector.memset(degree[:, :, TOP, 0, :], 6.0)
        nc.vector.memset(degree[:, :, BOTTOM, GROUP_ROWS - 1, :], 6.0)
        for kind, row in ((TOP, 0), (BOTTOM, GROUP_ROWS - 1)):
            nc.vector.memset(degree[:, 0, kind, row, 0:1], 4.0)
            nc.vector.memset(degree[:, 1, kind, row, HALF_COLS - 1 : HALF_COLS], 4.0)

        w_grouped = keep.tile([P, OUT_DIM, 4], BF16, align_bytes=64)
        w_codes = keep.tile([P, OUT_DIM], U32, align_bytes=64)
        w_scales = keep.tile([P, OUT_DIM], U8, align_bytes=64)
        nc.vector.tensor_copy(out=w_grouped[:], in_=w_raw[:].rearrange("q t c -> q c t"))
        nc.vector.quantize_mx(
            out=w_codes[:].bitcast(FP8X4), scales=w_scales[:], in_=w_grouped[:].rearrange("q c t -> q (c t)")
        )

        h_words = h_sb[:].bitcast(F32).rearrange("p (j t u w) -> p j t u w", j=CHUNKS, t=PER_PART, u=2)
        h_grouped = keep.tile([P, NODES * 4], BF16, align_bytes=64)
        h_grouped_words = h_grouped[:].bitcast(F32).rearrange(
            "q (j t p u) -> q j t p u", j=CHUNKS, t=PER_PART, u=2
        )
        h_codes = keep.tile([P, NODES], U32, align_bytes=64)
        h_scales = keep.tile([P, NODES], U8, align_bytes=64)
        stats = keep.tile([P, CHUNKS, 6], F32)
        y = []
        half = CHUNK // 2

        def turn_and_quantise(j):
            for h in range(2):
                h_t = psum.tile([P, 2, 2, P], F32, tag="bank")
                for t in range(2):
                    for u in range(2):
                        nc.tensor.transpose(h_t[:, t, u, :], h_words[:, j, 2 * h + t, u, :], ident[:])
                nc.scalar.copy(
                    out=h_grouped_words[:, j, 2 * h : 2 * h + 2, :, :],
                    in_=h_t[:].rearrange("q t u p -> q t p u"),
                )
                first = j * CHUNK + h * half
                nc.vector.quantize_mx(
                    out=h_codes[:, first : first + half].bitcast(FP8X4),
                    scales=h_scales[:, first : first + half],
                    in_=h_grouped[:, 4 * first : 4 * (first + half)],
                )

        def multiply(j):
            y.append(psum.tile([P, CHUNK], F32, tag="bank", name="y%d" % j))
            nc.tensor.matmul_mx(
                out=y[j][:],
                lhsT=w_codes[:].bitcast(FP8X4),
                lhsT_scale=w_scales[:],
                rhs=h_codes[:, j * CHUNK : (j + 1) * CHUNK].bitcast(FP8X4),
                rhs_scale=h_scales[:, j * CHUNK : (j + 1) * CHUNK],
                start=True,
                stop=True,
            )
            nc.vector.bn_stats(out=stats[:, j, :], in_=y[j][:])

        for j in range(CHUNKS):
            turn_and_quantise(j)
        for j in range(CHUNKS):
            multiply(j)

        gamma_d = keep.tile([P, 1], F32)
        minus_gamma_d = keep.tile([P, 1], F32)
        beta_d = keep.tile([P, 1], F32)
        nc.gpsimd.tensor_scalar_mul(out=gamma_d[:], in0=gamma_bf[:], scalar1=D_INSIDE)
        nc.gpsimd.tensor_scalar_mul(out=minus_gamma_d[:], in0=gamma_bf[:], scalar1=-D_INSIDE)
        nc.gpsimd.tensor_scalar_mul(out=beta_d[:], in0=beta_bf[:], scalar1=D_INSIDE)

        degree_t = [psum.tile([P, 3, P], F32, tag="bank", name="degree_t%d" % par) for par in range(2)]
        for par in range(2):
            for kind in (TOP, MIDDLE, BOTTOM):
                nc.tensor.transpose(
                    degree_t[par][:, kind, :], degree[:, par, kind, :, :].rearrange("f r m -> f (r m)"), ident[:]
                )

        mean_var = keep.tile([P, 2], F32)
        nc.vector.bn_aggr(out=mean_var[:], in_=stats[:].rearrange("f j s -> f (j s)"))
        rstd = keep.tile([P, 1], F32)
        minus_mean_gamma_d = keep.tile([P, 1], F32)
        scale = keep.tile([P, 1], F32)
        bias = keep.tile([P, 1], F32)
        nc.scalar.activation(out=rstd[:], in_=mean_var[:, 1:2], func=ACT.Abs_reciprocal_sqrt, bias=eps_bn[:])
        nc.vector.tensor_mul(out=minus_mean_gamma_d[:], in0=mean_var[:, 0:1], in1=minus_gamma_d[:])
        nc.vector.tensor_mul(out=scale[:], in0=gamma_d[:], in1=rstd[:])
        nc.vector.scalar_tensor_tensor(
            out=bias[:], in0=minus_mean_gamma_d[:], scalar=rstd[:], in1=beta_d[:], op0=ALU.mult, op1=ALU.add
        )

        last = COLS + 1
        for j in range(CHUNKS):
            rows = slice((j % 2) * CHUNK_ROWS, (j % 2 + 1) * CHUNK_ROWS)
            nc.scalar.activation(
                out=relu_d[j // 2][:, rows, 1:last].rearrange("f r (q t) -> f r q t", t=PER_PART),
                in_=y[j][:].rearrange("f (t r q) -> f r q t", t=PER_PART, r=CHUNK_ROWS),
                func=ACT.Relu,
                scale=scale[:],
                bias=bias[:],
            )
        d_out = keep.tile([P, 3, 2], F32)
        for par in range(2):
            nc.scalar.activation(
                out=d_out[:, :, par], in_=degree_t[par][:, :, 0], func=ACT.Abs_reciprocal_sqrt, bias=eps_deg[:]
            )

        pair = keep.tile([P, CHUNKS, CHUNK_ROWS, HALF_COLS], F32)

        def border(j):
            x = relu_d[j // 2]
            edge_row = 0 if j % 2 == 0 else ROWS - 1
            other_rows = slice(1, CHUNK_ROWS) if j % 2 == 0 else slice(CHUNK_ROWS, ROWS - 1)
            for region, factor in (
                (x[:, edge_row, 2 : last - 1], D_EDGE / D_INSIDE),
                (x[:, other_rows, 1 : last : COLS - 1], D_EDGE / D_INSIDE),
                (x[:, edge_row, 1 : last : COLS - 1], D_CORNER / D_INSIDE),
            ):
                nc.vector.tensor_scalar_mul(out=region, in0=region, scalar1=factor)

        border(0)
        for j in range(CHUNKS):
            x = relu_d[j // 2]
            rows = slice((j % 2) * CHUNK_ROWS, (j % 2 + 1) * CHUNK_ROWS)
            padded_rows = slice(1 + (j % 2) * CHUNK_ROWS, 1 + (j % 2 + 1) * CHUNK_ROWS)
            nc.vector.tensor_add(out=pair[:, j, :, :], in0=x[:, rows, 1:last:2], in1=x[:, rows, 2 : last + 1 : 2])
            nc.vector.tensor_add(
                out=col_sums[j // 2][:, 0, padded_rows, :], in0=pair[:, j, :, :], in1=x[:, rows, 0 : last - 1 : 2]
            )
            if j + 1 < CHUNKS:
                border(j + 1)
            nc.vector.tensor_add(
                out=col_sums[j // 2][:, 1, padded_rows, :], in0=pair[:, j, :, :], in1=x[:, rows, 3 : last + 1 : 2]
            )

        out_sb = keep.tile([P, GROUPS, 2, OUT_DIM], F32)
        for g in range(GROUPS):
            top = (g % GROUPS_PER_IMAGE) * GROUP_ROWS
            for par in range(2):
                box_t = psum.tile([P, OUT_DIM], F32, tag="bank")
                for dr in range(3):
                    nc.tensor.matmul(
                        out=box_t[:],
                        lhsT=col_sums[g // GROUPS_PER_IMAGE][:, par, top + dr : top + dr + GROUP_ROWS, :].rearrange(
                            "f r m -> f (r m)"
                        ),
                        rhs=ident[:],
                        is_transpose=True,
                        start=(dr == 0),
                        stop=(dr == 2),
                    )
                d_col = d_out[:, group_kind(g), par : par + 1]
                if par == 0:
                    nc.scalar.activation(out=out_sb[:, g, par, :], in_=box_t[:], func=ACT.Copy, scale=d_col)
                else:
                    nc.vector.tensor_scalar_mul(out=out_sb[:, g, par, :], in0=box_t[:], scalar1=d_col)
            nc.sync.dma_start(out=out_groups[:, g, :], in_=out_sb[:, g, :, :].rearrange("p two f -> p (two f)"))
